import numpy as np
import ml_dtypes


def mxq(x, axis, fmt="e4m3"):
    dtype, down = {"e4m3": (ml_dtypes.float8_e4m3fn, 7), "e5m2": (ml_dtypes.float8_e5m2, 14)}[fmt]
    v = np.moveaxis(np.asarray(x, np.float32).astype(ml_dtypes.bfloat16).astype(np.float64), axis, -1)
    blocks = v.reshape(v.shape[:-1] + (-1, 32))
    amax = np.abs(blocks).max(-1, keepdims=True)
    byte = np.maximum(np.where(amax > 0, np.frexp(amax)[1] - 1 + 127, 0) - down, 1)
    scale = np.exp2(byte - 127.0)
    codes = (blocks / scale).astype(np.float32).astype(dtype).astype(np.float64)
    return np.moveaxis((codes * scale).reshape(v.shape), -1, axis)


WIDE = False


def mx_kscale(k):
    if not WIDE:
        return np.ones(k)
    levels = np.array([10, -10, 5, -5, 0])
    a = np.random.permutation(np.resize(levels, k // 512 * 4)).reshape(k // 512, 4)
    idx = np.arange(k)
    return np.exp2(a[idx // 512, idx % 128 // 32])


BF16 = ml_dtypes.bfloat16


def bf(x):
    return np.asarray(x, np.float32).astype(BF16)


def f64(x):
    return np.asarray(x).astype(np.float64)


E2M1 = np.array([0.0, 0.5, 1.0, 1.5, 2.0, 3.0, 4.0, 6.0, -0.0, -0.5, -1.0, -1.5, -2.0, -3.0, -4.0, -6.0])


def pack_weight(w, fmt):
    k, n = w.shape
    w = f64(bf(w)).reshape(k // 32, 32, n)
    amax = np.abs(w).max(1)
    if fmt == "e4m3":
        byte = np.frexp(amax)[1] - 1 + 127 - 7
    else:
        mant, ex = np.frexp(amax / 6.0)
        byte = np.where(mant > 0.5, ex, ex - 1) + 127
    byte = np.clip(np.where(amax > 0, byte, 1), 1, 254)
    scaled = (w * np.exp2(127.0 - byte)[:, None, :]).reshape(k, n).astype(np.float32)
    by_word = np.ascontiguousarray(scaled.reshape(k // 512, 128, 4, n).transpose(0, 1, 3, 2))
    if fmt == "e4m3":
        words = by_word.astype(ml_dtypes.float8_e4m3fn).view(np.uint8)
    else:
        c = by_word.astype(ml_dtypes.float4_e2m1fn).view(np.uint8) & 0xF
        words = c[..., 0::2] | (c[..., 1::2] << 4)
    return np.ascontiguousarray(words), np.ascontiguousarray(byte.astype(np.uint8).reshape(k // 512, 16, n))


def unpack_weight(words, scales, fmt):
    g, p, n, _ = words.shape
    if fmt == "e4m3":
        vals = np.ascontiguousarray(words).view(ml_dtypes.float8_e4m3fn).astype(np.float64)
    else:
        nib = np.empty((g, p, n, 4), np.uint8)
        nib[..., 0::2] = words & 0xF
        nib[..., 1::2] = words >> 4
        vals = E2M1[nib]
    vals = vals * np.repeat(np.exp2(scales.astype(np.float64) - 127.0), 8, axis=1)[..., None]
    return vals.transpose(0, 1, 3, 2).reshape(g * 512, n)

def pack4(w):
    words, scales = pack_weight(w, "e2m1")
    return words.reshape(words.shape[0], 128, -1), scales


def unpack4(words, scales):
    return unpack_weight(words.reshape(words.shape[0], 128, -1, 2), scales, "e2m1")


S, N, C, O = 9, 128, 512, 4096
K = S * C


def setup_inputs():
    s = mx_kscale(K).reshape(S, C)
    inp = {f"x{i}": bf(np.random.standard_normal((N, C)) * s[i]) for i in range(S)}
    stack = (np.random.standard_normal((S, O, C)) / np.sqrt(K) / s[:, None, :]).swapaxes(1, 2)
    cat = stack.reshape(-1, O)
    words, scales = pack4(cat)
    inp["weights_words"] = words
    inp["weights_scales"] = scales
    inp["bias"] = bf(np.random.standard_normal((S, O)) * 0.3)
    return inp


def reference(x0, x1, x2, x3, x4, x5, x6, x7, x8, weights_words, weights_scales, bias):
    xs = np.stack([f64(x0), f64(x1), f64(x2), f64(x3), f64(x4), f64(x5), f64(x6), f64(x7), f64(x8)], axis=0)
    xc = xs.transpose(1, 0, 2).reshape(N, K)
    wc = unpack4(weights_words, weights_scales).reshape(S, C, O).reshape(K, O)
    out = mxq(xc, 1, "e4m3") @ wc
    out = out + np.sum(f64(bias), axis=0)
    return out

@@ -1,0 +1,113 @@
+import concourse.mybir as mybir
+from concourse.masks import make_identity
+
+F32 = mybir.dt.float32
+BF16 = mybir.dt.bfloat16
+I32 = mybir.dt.int32
+U32 = mybir.dt.uint32
+U8 = mybir.dt.uint8
+FP8X4 = mybir.dt.float8_e4m3fn_x4
+FP4X4 = mybir.dt.float4_e2m1fn_x4
+
+P = 128
+PACK = 4
+SLOTS = 9
+TOKENS = 128
+CHANNELS = P * PACK
+OUTS = 4096
+BANK_COLS = 512
+BANKS = OUTS // BANK_COLS
+HALF_BANKS = BANKS // 2
+STORE_BANKS = 2
+SCALE_SLOTS = 3
+WORD_BYTES = 2
+
+FLOPS = 2 * TOKENS * SLOTS * CHANNELS * OUTS
+
+
+def tile_scattervertical_w_e_kernel(
+    tc, x0, x1, x2, x3, x4, x5, x6, x7, x8, weights_words, weights_scales, bias, out
+):
+    nc = tc.nc
+    xs = [x0, x1, x2, x3, x4, x5, x6, x7, x8]
+
+    with tc.tile_pool(name="keep", bufs=1) as keep, tc.psum_pool(name="psum", bufs=1) as psum, tc.manual_schedule():
+        x_sb = keep.tile([P, SLOTS, CHANNELS], BF16)
+        grouped = keep.tile([P, SLOTS, TOKENS, PACK], BF16, align_bytes=64)
+        x_codes = keep.tile([P, SLOTS, TOKENS], U32, align_bytes=64)
+        x_scales = keep.tile([P, SLOTS, TOKENS], U8, align_bytes=64)
+        w_words = keep.tile([P, SLOTS, OUTS * WORD_BYTES], U8, align_bytes=64)
+        w_scales = keep.tile([P, SLOTS, OUTS], U8, align_bytes=64)
+        bias_rows = keep.tile([P, OUTS], BF16)
+        ones = keep.tile([P, P], BF16)
+        identity = keep.tile([P, P], F32)
+        out_sb = keep.tile([P, OUTS], F32)
+
+        nc.vector.memset(bias_rows[:].bitcast(I32), 0)
+        for first in range(0, SLOTS, SCALE_SLOTS):
+            nc.vector.memset(w_scales[:, first : first + SCALE_SLOTS, :].bitcast(I32), 0)
+        make_identity(nc, identity[:])
+        nc.gpsimd.memset(ones[:], 1.0)
+
+        for g in range(SLOTS):
+            nc.sync.dma_start(out=x_sb[:, g, :], in_=xs[g])
+        nc.sync.dma_start(out=bias_rows[0:SLOTS, :], in_=bias)
+        scales_by_row = weights_scales.rearrange("g q n -> q g n")
+        for first in range(0, SLOTS, SCALE_SLOTS):
+            for b in range(2):
+                for r in range(PACK):
+                    nc.sync.dma_start(
+                        out=w_scales[32 * b + r : P : 64, first : first + SCALE_SLOTS, :].bitcast(I32),
+                        in_=scales_by_row[4 * b + r : 16 : 8, first : first + SCALE_SLOTS, :].bitcast(I32),
+                    )
+        for half in range(2):
+            lo = half * HALF_BANKS * BANK_COLS * WORD_BYTES
+            hi = lo + HALF_BANKS * BANK_COLS * WORD_BYTES
+            for g in range(SLOTS):
+                nc.sync.dma_start(
+                    out=w_words[:, g, lo:hi].bitcast(I32), in_=weights_words[g, :, lo:hi].bitcast(I32)
+                )
+
+        x_pairs = x_sb[:].bitcast(F32)
+        for g in range(SLOTS):
+            turned = psum.tile([P, 2, TOKENS], F32, tag="bank%d" % (g % BANKS), name="turned")
+            for u in range(2):
+                nc.tensor.transpose(turned[:, u, :], x_pairs[:, g, u : CHANNELS // 2 : 2], identity[:])
+            nc.scalar.copy(
+                out=grouped[:, g].rearrange("p n t -> p (n t)").bitcast(F32).rearrange("p (n u) -> p n u", u=2),
+                in_=turned[:].rearrange("p u n -> p n u"),
+            )
+            nc.vector.quantize_mx(
+                out=x_codes[:, g, :].bitcast(FP8X4),
+                scales=x_scales[:, g, :],
+                in_=grouped[:, g].rearrange("p n t -> p (n t)"),
+            )
+
+        for j in range(BANKS):
+            cols = slice(j * BANK_COLS, (j + 1) * BANK_COLS)
+            bias_sum = psum.tile([P, BANK_COLS], F32, tag="bank%d" % j, name="bias_sum")
+            nc.tensor.matmul(out=bias_sum[:], lhsT=ones[:], rhs=bias_rows[:, cols], start=True, stop=True)
+            nc.scalar.copy(out=out_sb[:, cols], in_=bias_sum[:])
+
+        for half in range(2):
+            banks = range(half * HALF_BANKS, (half + 1) * HALF_BANKS)
+            acc = {}
+            for j in banks:
+                acc[j] = psum.tile([P, BANK_COLS], F32, tag="bank%d" % j, name="acc")
+            for g in range(SLOTS):
+                for j in banks:
+                    nc.tensor.matmul_mx(
+                        out=acc[j][:],
+                        lhsT=x_codes[:, g, :].bitcast(FP8X4),
+                        lhsT_scale=x_scales[:, g, :],
+                        rhs=w_words[:, g, j * BANK_COLS * WORD_BYTES : (j + 1) * BANK_COLS * WORD_BYTES].bitcast(FP4X4),
+                        rhs_scale=w_scales[:, g, j * BANK_COLS : (j + 1) * BANK_COLS],
+                        start=(g == 0),
+                        stop=(g == SLOTS - 1),
+                    )
+            for j in banks:
+                cols = slice(j * BANK_COLS, (j + 1) * BANK_COLS)
+                nc.vector.tensor_add(out=out_sb[:, cols], in0=acc[j][:], in1=out_sb[:, cols])
+                if j % STORE_BANKS == STORE_BANKS - 1:
+                    leaving = slice((j + 1 - STORE_BANKS) * BANK_COLS, (j + 1) * BANK_COLS)
+                    nc.sync.dma_start(out=out[:, leaving], in_=out_sb[:, leaving])

@@ -43,23 +43,23 @@ def tile_scattervertical_w_e_kernel(
         identity = keep.tile([P, P], F32)
         out_sb = keep.tile([P, OUTS], F32)
 
-        nc.vector.memset(bias_rows[:].bitcast(I32), 0)
         for first in range(0, SLOTS, SCALE_SLOTS):
             nc.vector.memset(w_scales[:, first : first + SCALE_SLOTS, :].bitcast(I32), 0)
+        nc.vector.memset(bias_rows[:].bitcast(I32), 0)
+        nc.vector.memset(ones[:], 1.0)
         make_identity(nc, identity[:])
-        nc.gpsimd.memset(ones[:], 1.0)
+
+        scales_by_row = weights_scales.rearrange("g q n -> q g n")
+        for first in range(0, SLOTS, SCALE_SLOTS):
+            for r in range(PACK):
+                nc.gpsimd.dma_start(
+                    out=w_scales[r : P : 32, first : first + SCALE_SLOTS, :].bitcast(F32),
+                    in_=scales_by_row[r : 16 : PACK, first : first + SCALE_SLOTS, :].bitcast(F32),
+                )
 
         for g in range(SLOTS):
             nc.sync.dma_start(out=x_sb[:, g, :], in_=xs[g])
         nc.sync.dma_start(out=bias_rows[0:SLOTS, :], in_=bias)
-        scales_by_row = weights_scales.rearrange("g q n -> q g n")
-        for first in range(0, SLOTS, SCALE_SLOTS):
-            for b in range(2):
-                for r in range(PACK):
-                    nc.sync.dma_start(
-                        out=w_scales[32 * b + r : P : 64, first : first + SCALE_SLOTS, :].bitcast(I32),
-                        in_=scales_by_row[4 * b + r : 16 : 8, first : first + SCALE_SLOTS, :].bitcast(I32),
-                    )
         for half in range(2):
             lo = half * HALF_BANKS * BANK_COLS * WORD_BYTES
             hi = lo + HALF_BANKS * BANK_COLS * WORD_BYTES

@@ -17,7 +17,7 @@ CHANNELS = P * PACK
 OUTS = 4096
 BANK_COLS = 512
 BANKS = OUTS // BANK_COLS
-HALF_BANKS = BANKS // 2
+FIRST_BANKS = 6
 STORE_BANKS = 2
 SCALE_SLOTS = 3
 WORD_BYTES = 2
@@ -43,26 +43,27 @@ def tile_scattervertical_w_e_kernel(
         identity = keep.tile([P, P], F32)
         out_sb = keep.tile([P, OUTS], F32)
 
+        nc.vector.memset(bias_rows[:].bitcast(I32), 0)
         for first in range(0, SLOTS, SCALE_SLOTS):
             nc.vector.memset(w_scales[:, first : first + SCALE_SLOTS, :].bitcast(I32), 0)
-        nc.vector.memset(bias_rows[:].bitcast(I32), 0)
-        nc.vector.memset(ones[:], 1.0)
         make_identity(nc, identity[:])
-
-        scales_by_row = weights_scales.rearrange("g q n -> q g n")
-        for first in range(0, SLOTS, SCALE_SLOTS):
-            for r in range(PACK):
-                nc.gpsimd.dma_start(
-                    out=w_scales[r : P : 32, first : first + SCALE_SLOTS, :].bitcast(F32),
-                    in_=scales_by_row[r : 16 : PACK, first : first + SCALE_SLOTS, :].bitcast(F32),
-                )
+        nc.gpsimd.memset(ones[:], 1.0)
 
         for g in range(SLOTS):
             nc.sync.dma_start(out=x_sb[:, g, :], in_=xs[g])
-        nc.sync.dma_start(out=bias_rows[0:SLOTS, :], in_=bias)
-        for half in range(2):
-            lo = half * HALF_BANKS * BANK_COLS * WORD_BYTES
-            hi = lo + HALF_BANKS * BANK_COLS * WORD_BYTES
+        nc.sync.dma_start(out=bias_rows[4 : 4 + 8 * SLOTS : 8, :], in_=bias)
+        scales_by_row = weights_scales.rearrange("g q n -> q g n")
+        for first in range(0, SLOTS, SCALE_SLOTS):
+            for b in range(2):
+                for r in range(PACK):
+                    nc.sync.dma_start(
+                        out=w_scales[32 * b + r : P : 64, first : first + SCALE_SLOTS, :].bitcast(I32),
+                        in_=scales_by_row[4 * b + r : 16 : 8, first : first + SCALE_SLOTS, :].bitcast(I32),
+                    )
+        parts = ((0, FIRST_BANKS), (FIRST_BANKS, BANKS))
+        for first_bank, end_bank in parts:
+            lo = first_bank * BANK_COLS * WORD_BYTES
+            hi = end_bank * BANK_COLS * WORD_BYTES
             for g in range(SLOTS):
                 nc.sync.dma_start(
                     out=w_words[:, g, lo:hi].bitcast(I32), in_=weights_words[g, :, lo:hi].bitcast(I32)
@@ -89,8 +90,8 @@ def tile_scattervertical_w_e_kernel(
             nc.tensor.matmul(out=bias_sum[:], lhsT=ones[:], rhs=bias_rows[:, cols], start=True, stop=True)
             nc.scalar.copy(out=out_sb[:, cols], in_=bias_sum[:])
 
-        for half in range(2):
-            banks = range(half * HALF_BANKS, (half + 1) * HALF_BANKS)
+        for first_bank, end_bank in parts:
+            banks = range(first_bank, end_bank)
             acc = {}
             for j in banks:
                 acc[j] = psum.tile([P, BANK_COLS], F32, tag="bank%d" % j, name="acc")

@@ -19,7 +19,7 @@ BANK_COLS = 512
 BANKS = OUTS // BANK_COLS
 FIRST_BANKS = 6
 STORE_BANKS = 2
-SCALE_SLOTS = 3
+HOLD_BYTES = 16
 WORD_BYTES = 2
 
 FLOPS = 2 * TOKENS * SLOTS * CHANNELS * OUTS
@@ -43,31 +43,35 @@ def tile_scattervertical_w_e_kernel(
         identity = keep.tile([P, P], F32)
         out_sb = keep.tile([P, OUTS], F32)
 
+        nc.vector.memset(w_scales[:].rearrange("p g n -> p (g n)").bitcast(I32), 0)
         nc.vector.memset(bias_rows[:].bitcast(I32), 0)
-        for first in range(0, SLOTS, SCALE_SLOTS):
-            nc.vector.memset(w_scales[:, first : first + SCALE_SLOTS, :].bitcast(I32), 0)
         make_identity(nc, identity[:])
         nc.gpsimd.memset(ones[:], 1.0)
 
         for g in range(SLOTS):
             nc.sync.dma_start(out=x_sb[:, g, :], in_=xs[g])
-        nc.sync.dma_start(out=bias_rows[4 : 4 + 8 * SLOTS : 8, :], in_=bias)
-        scales_by_row = weights_scales.rearrange("g q n -> q g n")
-        for first in range(0, SLOTS, SCALE_SLOTS):
-            for b in range(2):
-                for r in range(PACK):
-                    nc.sync.dma_start(
-                        out=w_scales[32 * b + r : P : 64, first : first + SCALE_SLOTS, :].bitcast(I32),
-                        in_=scales_by_row[4 * b + r : 16 : 8, first : first + SCALE_SLOTS, :].bitcast(I32),
-                    )
         parts = ((0, FIRST_BANKS), (FIRST_BANKS, BANKS))
-        for first_bank, end_bank in parts:
-            lo = first_bank * BANK_COLS * WORD_BYTES
-            hi = end_bank * BANK_COLS * WORD_BYTES
-            for g in range(SLOTS):
+
+        def load_words(part, g):
+            lo = part[0] * BANK_COLS * WORD_BYTES
+            hi = part[1] * BANK_COLS * WORD_BYTES
+            nc.sync.dma_start(out=w_words[:, g, lo:hi].bitcast(I32), in_=weights_words[g, :, lo:hi].bitcast(I32))
+
+        load_words(parts[0], 0)
+        scales_by_row = weights_scales.rearrange("g q n -> q g n")
+        for b in range(2):
+            for r in range(PACK):
                 nc.sync.dma_start(
-                    out=w_words[:, g, lo:hi].bitcast(I32), in_=weights_words[g, :, lo:hi].bitcast(I32)
+                    out=w_scales[32 * b + r : P : 64, :, :].bitcast(I32),
+                    in_=scales_by_row[4 * b + r : 16 : 8, :, :].bitcast(I32),
                 )
+        nc.gpsimd.tensor_copy(
+            out=w_words[32:34, 1, 0:HOLD_BYTES].bitcast(I32), in_=w_scales[32:34, 0, 0:HOLD_BYTES].bitcast(I32)
+        )
+        for g in range(1, SLOTS):
+            load_words(parts[0], g)
+        for g in range(SLOTS):
+            load_words(parts[1], g)
 
         x_pairs = x_sb[:].bitcast(F32)
         for g in range(SLOTS):
@@ -84,11 +88,15 @@ def tile_scattervertical_w_e_kernel(
                 in_=grouped[:, g].rearrange("p n t -> p (n t)"),
             )
 
+        nc.scalar.dma_start(out=bias_rows[4 : 4 + 8 * SLOTS : 8, :], in_=bias)
         for j in range(BANKS):
             cols = slice(j * BANK_COLS, (j + 1) * BANK_COLS)
             bias_sum = psum.tile([P, BANK_COLS], F32, tag="bank%d" % j, name="bias_sum")
             nc.tensor.matmul(out=bias_sum[:], lhsT=ones[:], rhs=bias_rows[:, cols], start=True, stop=True)
-            nc.scalar.copy(out=out_sb[:, cols], in_=bias_sum[:])
+            if j % 2 == 0:
+                nc.vector.tensor_copy(out=out_sb[:, cols], in_=bias_sum[:])
+            else:
+                nc.scalar.copy(out=out_sb[:, cols], in_=bias_sum[:])
 
         for first_bank, end_bank in parts:
             banks = range(first_bank, end_bank)

@@ -18,9 +18,11 @@ OUTS = 4096
 BANK_COLS = 512
 BANKS = OUTS // BANK_COLS
 FIRST_BANKS = 6
-STORE_BANKS = 2
+STORE_BANKS = 3
+LAST_SLOTS = 3
 HOLD_BYTES = 16
 WORD_BYTES = 2
+BANK_BYTES = BANK_COLS * WORD_BYTES
 
 FLOPS = 2 * TOKENS * SLOTS * CHANNELS * OUTS
 
@@ -36,7 +38,8 @@ def tile_scattervertical_w_e_kernel(
         grouped = keep.tile([P, SLOTS, TOKENS, PACK], BF16, align_bytes=64)
         x_codes = keep.tile([P, SLOTS, TOKENS], U32, align_bytes=64)
         x_scales = keep.tile([P, SLOTS, TOKENS], U8, align_bytes=64)
-        w_words = keep.tile([P, SLOTS, OUTS * WORD_BYTES], U8, align_bytes=64)
+        w_first = keep.tile([P, SLOTS, FIRST_BANKS * BANK_BYTES], U8, align_bytes=64)
+        w_last = keep.tile([P, SLOTS, (BANKS - FIRST_BANKS) * BANK_BYTES], U8, align_bytes=64)
         w_scales = keep.tile([P, SLOTS, OUTS], U8, align_bytes=64)
         bias_rows = keep.tile([P, OUTS], BF16)
         ones = keep.tile([P, P], BF16)
@@ -52,12 +55,15 @@ def tile_scattervertical_w_e_kernel(
             nc.sync.dma_start(out=x_sb[:, g, :], in_=xs[g])
         parts = ((0, FIRST_BANKS), (FIRST_BANKS, BANKS))
 
-        def load_words(part, g):
-            lo = part[0] * BANK_COLS * WORD_BYTES
-            hi = part[1] * BANK_COLS * WORD_BYTES
-            nc.sync.dma_start(out=w_words[:, g, lo:hi].bitcast(I32), in_=weights_words[g, :, lo:hi].bitcast(I32))
+        words_by_row = weights_words.rearrange("g p n -> p g n")
 
-        load_words(parts[0], 0)
+        def load_words(tile, part, first_slot, end_slot):
+            nc.sync.dma_start(
+                out=tile[:, first_slot:end_slot, :].bitcast(I32),
+                in_=words_by_row[:, first_slot:end_slot, part[0] * BANK_BYTES : part[1] * BANK_BYTES].bitcast(I32),
+            )
+
+        load_words(w_first, parts[0], 0, 1)
         scales_by_row = weights_scales.rearrange("g q n -> q g n")
         for b in range(2):
             for r in range(PACK):
@@ -66,12 +72,12 @@ def tile_scattervertical_w_e_kernel(
                     in_=scales_by_row[4 * b + r : 16 : 8, :, :].bitcast(I32),
                 )
         nc.gpsimd.tensor_copy(
-            out=w_words[32:34, 1, 0:HOLD_BYTES].bitcast(I32), in_=w_scales[32:34, 0, 0:HOLD_BYTES].bitcast(I32)
+            out=w_first[32:34, 1, 0:HOLD_BYTES].bitcast(I32), in_=w_scales[32:34, 0, 0:HOLD_BYTES].bitcast(I32)
         )
         for g in range(1, SLOTS):
-            load_words(parts[0], g)
-        for g in range(SLOTS):
-            load_words(parts[1], g)
+            load_words(w_first, parts[0], g, g + 1)
+        for g in range(0, SLOTS, LAST_SLOTS):
+            load_words(w_last, parts[1], g, g + LAST_SLOTS)
 
         x_pairs = x_sb[:].bitcast(F32)
         for g in range(SLOTS):
@@ -98,7 +104,7 @@ def tile_scattervertical_w_e_kernel(
             else:
                 nc.scalar.copy(out=out_sb[:, cols], in_=bias_sum[:])
 
-        for first_bank, end_bank in parts:
+        for words, (first_bank, end_bank) in zip((w_first, w_last), parts):
             banks = range(first_bank, end_bank)
             acc = {}
             for j in banks:
@@ -109,7 +115,7 @@ def tile_scattervertical_w_e_kernel(
                         out=acc[j][:],
                         lhsT=x_codes[:, g, :].bitcast(FP8X4),
                         lhsT_scale=x_scales[:, g, :],
-                        rhs=w_words[:, g, j * BANK_COLS * WORD_BYTES : (j + 1) * BANK_COLS * WORD_BYTES].bitcast(FP4X4),
+                        rhs=words[:, g, (j - first_bank) * BANK_BYTES : (j + 1 - first_bank) * BANK_BYTES].bitcast(FP4X4),
                         rhs_scale=w_scales[:, g, j * BANK_COLS : (j + 1) * BANK_COLS],
                         start=(g == 0),
                         stop=(g == SLOTS - 1),
@@ -117,6 +123,6 @@ def tile_scattervertical_w_e_kernel(
             for j in banks:
                 cols = slice(j * BANK_COLS, (j + 1) * BANK_COLS)
                 nc.vector.tensor_add(out=out_sb[:, cols], in0=acc[j][:], in1=out_sb[:, cols])
-                if j % STORE_BANKS == STORE_BANKS - 1:
-                    leaving = slice((j + 1 - STORE_BANKS) * BANK_COLS, (j + 1) * BANK_COLS)
+                if j % STORE_BANKS == STORE_BANKS - 1 or j == BANKS - 1:
+                    leaving = slice((j - j % STORE_BANKS) * BANK_COLS, (j + 1) * BANK_COLS)
                     nc.sync.dma_start(out=out[:, leaving], in_=out_sb[:, leaving])

@@ -18,8 +18,8 @@ OUTS = 4096
 BANK_COLS = 512
 BANKS = OUTS // BANK_COLS
 FIRST_BANKS = 6
-STORE_BANKS = 3
-LAST_SLOTS = 3
+STORE_BANKS = 2
+LAST_SLOTS = 2
 HOLD_BYTES = 16
 WORD_BYTES = 2
 BANK_BYTES = BANK_COLS * WORD_BYTES
@@ -77,7 +77,7 @@ def tile_scattervertical_w_e_kernel(
         for g in range(1, SLOTS):
             load_words(w_first, parts[0], g, g + 1)
         for g in range(0, SLOTS, LAST_SLOTS):
-            load_words(w_last, parts[1], g, g + LAST_SLOTS)
+            load_words(w_last, parts[1], g, min(g + LAST_SLOTS, SLOTS))
 
         x_pairs = x_sb[:].bitcast(F32)
         for g in range(SLOTS):

@@ -18,7 +18,8 @@ OUTS = 4096
 BANK_COLS = 512
 BANKS = OUTS // BANK_COLS
 FIRST_BANKS = 6
-STORE_BANKS = 2
+STORE_BANKS = (2, 1)
+BANK_SLOTS = (1, 2)
 LAST_SLOTS = 2
 HOLD_BYTES = 16
 WORD_BYTES = 2
@@ -79,6 +80,8 @@ def tile_scattervertical_w_e_kernel(
         for g in range(0, SLOTS, LAST_SLOTS):
             load_words(w_last, parts[1], g, min(g + LAST_SLOTS, SLOTS))
 
+        nc.scalar.dma_start(out=bias_rows[4 : 4 + 8 * SLOTS : 8, :], in_=bias)
+
         x_pairs = x_sb[:].bitcast(F32)
         for g in range(SLOTS):
             turned = psum.tile([P, 2, TOKENS], F32, tag="bank%d" % (g % BANKS), name="turned")
@@ -94,7 +97,6 @@ def tile_scattervertical_w_e_kernel(
                 in_=grouped[:, g].rearrange("p n t -> p (n t)"),
             )
 
-        nc.scalar.dma_start(out=bias_rows[4 : 4 + 8 * SLOTS : 8, :], in_=bias)
         for j in range(BANKS):
             cols = slice(j * BANK_COLS, (j + 1) * BANK_COLS)
             bias_sum = psum.tile([P, BANK_COLS], F32, tag="bank%d" % j, name="bias_sum")
@@ -104,25 +106,31 @@ def tile_scattervertical_w_e_kernel(
             else:
                 nc.scalar.copy(out=out_sb[:, cols], in_=bias_sum[:])
 
-        for words, (first_bank, end_bank) in zip((w_first, w_last), parts):
+        for words, (first_bank, end_bank), bank_slots, store_banks in zip((w_first, w_last), parts, BANK_SLOTS, STORE_BANKS):
             banks = range(first_bank, end_bank)
             acc = {}
             for j in banks:
                 acc[j] = psum.tile([P, BANK_COLS], F32, tag="bank%d" % j, name="acc")
-            for g in range(SLOTS):
+            order = []
+            for g in range(SLOTS - bank_slots):
                 for j in banks:
-                    nc.tensor.matmul_mx(
-                        out=acc[j][:],
-                        lhsT=x_codes[:, g, :].bitcast(FP8X4),
-                        lhsT_scale=x_scales[:, g, :],
-                        rhs=words[:, g, (j - first_bank) * BANK_BYTES : (j + 1 - first_bank) * BANK_BYTES].bitcast(FP4X4),
-                        rhs_scale=w_scales[:, g, j * BANK_COLS : (j + 1) * BANK_COLS],
-                        start=(g == 0),
-                        stop=(g == SLOTS - 1),
-                    )
+                    order.append((g, j))
+            for j in banks:
+                for g in range(SLOTS - bank_slots, SLOTS):
+                    order.append((g, j))
+            for g, j in order:
+                nc.tensor.matmul_mx(
+                    out=acc[j][:],
+                    lhsT=x_codes[:, g, :].bitcast(FP8X4),
+                    lhsT_scale=x_scales[:, g, :],
+                    rhs=words[:, g, (j - first_bank) * BANK_BYTES : (j + 1 - first_bank) * BANK_BYTES].bitcast(FP4X4),
+                    rhs_scale=w_scales[:, g, j * BANK_COLS : (j + 1) * BANK_COLS],
+                    start=(g == 0),
+                    stop=(g == SLOTS - 1),
+                )
             for j in banks:
                 cols = slice(j * BANK_COLS, (j + 1) * BANK_COLS)
                 nc.vector.tensor_add(out=out_sb[:, cols], in0=acc[j][:], in1=out_sb[:, cols])
-                if j % STORE_BANKS == STORE_BANKS - 1 or j == BANKS - 1:
-                    leaving = slice((j - j % STORE_BANKS) * BANK_COLS, (j + 1) * BANK_COLS)
+                if j % store_banks == store_banks - 1:
+                    leaving = slice((j + 1 - store_banks) * BANK_COLS, (j + 1) * BANK_COLS)
                     nc.sync.dma_start(out=out[:, leaving], in_=out_sb[:, leaving])

import concourse.mybir as mybir
from concourse.masks import make_identity

F32 = mybir.dt.float32
BF16 = mybir.dt.bfloat16
I32 = mybir.dt.int32
U32 = mybir.dt.uint32
U8 = mybir.dt.uint8
FP8X4 = mybir.dt.float8_e4m3fn_x4
FP4X4 = mybir.dt.float4_e2m1fn_x4

P = 128
PACK = 4
SLOTS = 9
TOKENS = 128
CHANNELS = P * PACK
OUTS = 4096
BANK_COLS = 512
BANKS = OUTS // BANK_COLS
FIRST_BANKS = 6
STORE_BANKS = (2, 1)
BANK_SLOTS = (1, 2)
LAST_SLOTS = 2
HOLD_BYTES = 16
WORD_BYTES = 2
BANK_BYTES = BANK_COLS * WORD_BYTES

FLOPS = 2 * TOKENS * SLOTS * CHANNELS * OUTS


def tile_scattervertical_w_e_kernel(
    tc, x0, x1, x2, x3, x4, x5, x6, x7, x8, weights_words, weights_scales, bias, out
):
    nc = tc.nc
    xs = [x0, x1, x2, x3, x4, x5, x6, x7, x8]

    with tc.tile_pool(name="keep", bufs=1) as keep, tc.psum_pool(name="psum", bufs=1) as psum, tc.manual_schedule():
        x_sb = keep.tile([P, SLOTS, CHANNELS], BF16)
        grouped = keep.tile([P, SLOTS, TOKENS, PACK], BF16, align_bytes=64)
        x_codes = keep.tile([P, SLOTS, TOKENS], U32, align_bytes=64)
        x_scales = keep.tile([P, SLOTS, TOKENS], U8, align_bytes=64)
        w_first = keep.tile([P, SLOTS, FIRST_BANKS * BANK_BYTES], U8, align_bytes=64)
        w_last = keep.tile([P, SLOTS, (BANKS - FIRST_BANKS) * BANK_BYTES], U8, align_bytes=64)
        w_scales = keep.tile([P, SLOTS, OUTS], U8, align_bytes=64)
        bias_rows = keep.tile([P, OUTS], BF16)
        ones = keep.tile([P, P], BF16)
        identity = keep.tile([P, P], F32)
        out_sb = keep.tile([P, OUTS], F32)

        nc.vector.memset(w_scales[:].rearrange("p g n -> p (g n)").bitcast(I32), 0)
        nc.vector.memset(bias_rows[:].bitcast(I32), 0)
        make_identity(nc, identity[:])
        nc.gpsimd.memset(ones[:], 1.0)

        for g in range(SLOTS):
            nc.sync.dma_start(out=x_sb[:, g, :], in_=xs[g])
        parts = ((0, FIRST_BANKS), (FIRST_BANKS, BANKS))

        words_by_row = weights_words.rearrange("g p n -> p g n")

        def load_words(tile, part, first_slot, end_slot):
            nc.sync.dma_start(
                out=tile[:, first_slot:end_slot, :].bitcast(I32),
                in_=words_by_row[:, first_slot:end_slot, part[0] * BANK_BYTES : part[1] * BANK_BYTES].bitcast(I32),
            )

        load_words(w_first, parts[0], 0, 1)
        scales_by_row = weights_scales.rearrange("g q n -> q g n")
        for b in range(2):
            for r in range(PACK):
                nc.sync.dma_start(
                    out=w_scales[32 * b + r : P : 64, :, :].bitcast(I32),
                    in_=scales_by_row[4 * b + r : 16 : 8, :, :].bitcast(I32),
                )
        nc.gpsimd.tensor_copy(
            out=w_first[32:34, 1, 0:HOLD_BYTES].bitcast(I32), in_=w_scales[32:34, 0, 0:HOLD_BYTES].bitcast(I32)
        )
        for g in range(1, SLOTS):
            load_words(w_first, parts[0], g, g + 1)
        for g in range(0, SLOTS, LAST_SLOTS):
            load_words(w_last, parts[1], g, min(g + LAST_SLOTS, SLOTS))

        nc.scalar.dma_start(out=bias_rows[4 : 4 + 8 * SLOTS : 8, :], in_=bias)

        x_pairs = x_sb[:].bitcast(F32)
        for g in range(SLOTS):
            turned = psum.tile([P, 2, TOKENS], F32, tag="bank%d" % (g % BANKS), name="turned")
            for u in range(2):
                nc.tensor.transpose(turned[:, u, :], x_pairs[:, g, u : CHANNELS // 2 : 2], identity[:])
            nc.scalar.copy(
                out=grouped[:, g].rearrange("p n t -> p (n t)").bitcast(F32).rearrange("p (n u) -> p n u", u=2),
                in_=turned[:].rearrange("p u n -> p n u"),
            )
            nc.vector.quantize_mx(
                out=x_codes[:, g, :].bitcast(FP8X4),
                scales=x_scales[:, g, :],
                in_=grouped[:, g].rearrange("p n t -> p (n t)"),
            )

        for j in range(BANKS):
            cols = slice(j * BANK_COLS, (j + 1) * BANK_COLS)
            bias_sum = psum.tile([P, BANK_COLS], F32, tag="bank%d" % j, name="bias_sum")
            nc.tensor.matmul(out=bias_sum[:], lhsT=ones[:], rhs=bias_rows[:, cols], start=True, stop=True)
            if j % 2 == 0:
                nc.vector.tensor_copy(out=out_sb[:, cols], in_=bias_sum[:])
            else:
                nc.scalar.copy(out=out_sb[:, cols], in_=bias_sum[:])

        for words, (first_bank, end_bank), bank_slots, store_banks in zip((w_first, w_last), parts, BANK_SLOTS, STORE_BANKS):
            banks = range(first_bank, end_bank)
            acc = {}
            for j in banks:
                acc[j] = psum.tile([P, BANK_COLS], F32, tag="bank%d" % j, name="acc")
            order = []
            for g in range(SLOTS - bank_slots):
                for j in banks:
                    order.append((g, j))
            for j in banks:
                for g in range(SLOTS - bank_slots, SLOTS):
                    order.append((g, j))
            for g, j in order:
                nc.tensor.matmul_mx(
                    out=acc[j][:],
                    lhsT=x_codes[:, g, :].bitcast(FP8X4),
                    lhsT_scale=x_scales[:, g, :],
                    rhs=words[:, g, (j - first_bank) * BANK_BYTES : (j + 1 - first_bank) * BANK_BYTES].bitcast(FP4X4),
                    rhs_scale=w_scales[:, g, j * BANK_COLS : (j + 1) * BANK_COLS],
                    start=(g == 0),
                    stop=(g == SLOTS - 1),
                )
            for j in banks:
                cols = slice(j * BANK_COLS, (j + 1) * BANK_COLS)
                nc.vector.tensor_add(out=out_sb[:, cols], in0=acc[j][:], in1=out_sb[:, cols])
                if j % store_banks == store_banks - 1:
                    leaving = slice((j + 1 - store_banks) * BANK_COLS, (j + 1) * BANK_COLS)
                    nc.sync.dma_start(out=out[:, leaving], in_=out_sb[:, leaving])
